import numpy as np
import ml_dtypes


def mxq(x, axis, fmt="e4m3"):
    dtype, down = {"e4m3": (ml_dtypes.float8_e4m3fn, 7), "e5m2": (ml_dtypes.float8_e5m2, 14)}[fmt]
    v = np.moveaxis(np.asarray(x, np.float32).astype(ml_dtypes.bfloat16).astype(np.float64), axis, -1)
    blocks = v.reshape(v.shape[:-1] + (-1, 32))
    amax = np.abs(blocks).max(-1, keepdims=True)
    byte = np.maximum(np.where(amax > 0, np.frexp(amax)[1] - 1 + 127, 0) - down, 1)
    scale = np.exp2(byte - 127.0)
    codes = (blocks / scale).astype(np.float32).astype(dtype).astype(np.float64)
    return np.moveaxis((codes * scale).reshape(v.shape), -1, axis)


WIDE = False


def mx_kscale(k):
    if not WIDE:
        return np.ones(k)
    levels = np.array([10, -10, 5, -5, 0])
    a = np.random.permutation(np.resize(levels, k // 512 * 4)).reshape(k // 512, 4)
    idx = np.arange(k)
    return np.exp2(a[idx // 512, idx % 128 // 32])


BF16 = ml_dtypes.bfloat16


def bf(x):
    return np.asarray(x, np.float32).astype(BF16)


def f64(x):
    return np.asarray(x).astype(np.float64)


E2M1 = np.array([0.0, 0.5, 1.0, 1.5, 2.0, 3.0, 4.0, 6.0, -0.0, -0.5, -1.0, -1.5, -2.0, -3.0, -4.0, -6.0])


def pack_weight(w, fmt):
    k, n = w.shape
    w = f64(bf(w)).reshape(k // 32, 32, n)
    amax = np.abs(w).max(1)
    if fmt == "e4m3":
        byte = np.frexp(amax)[1] - 1 + 127 - 7
    else:
        mant, ex = np.frexp(amax / 6.0)
        byte = np.where(mant > 0.5, ex, ex - 1) + 127
    byte = np.clip(np.where(amax > 0, byte, 1), 1, 254)
    scaled = (w * np.exp2(127.0 - byte)[:, None, :]).reshape(k, n).astype(np.float32)
    by_word = np.ascontiguousarray(scaled.reshape(k // 512, 128, 4, n).transpose(0, 1, 3, 2))
    if fmt == "e4m3":
        words = by_word.astype(ml_dtypes.float8_e4m3fn).view(np.uint8)
    else:
        c = by_word.astype(ml_dtypes.float4_e2m1fn).view(np.uint8) & 0xF
        words = c[..., 0::2] | (c[..., 1::2] << 4)
    return np.ascontiguousarray(words), np.ascontiguousarray(byte.astype(np.uint8).reshape(k // 512, 16, n))


def unpack_weight(words, scales, fmt):
    g, p, n, _ = words.shape
    if fmt == "e4m3":
        vals = np.ascontiguousarray(words).view(ml_dtypes.float8_e4m3fn).astype(np.float64)
    else:
        nib = np.empty((g, p, n, 4), np.uint8)
        nib[..., 0::2] = words & 0xF
        nib[..., 1::2] = words >> 4
        vals = E2M1[nib]
    vals = vals * np.repeat(np.exp2(scales.astype(np.float64) - 127.0), 8, axis=1)[..., None]
    return vals.transpose(0, 1, 3, 2).reshape(g * 512, n)


E, T, H, F = 2, 128, 2048, 2048


def silu(v):
    return v / (1.0 + np.exp(-v))


def setup_inputs():
    s, t = mx_kscale(H), mx_kscale(F)
    hidden_states = bf(np.random.standard_normal((E * T, H)) * s)
    gate_stack = np.random.standard_normal((E, H, F)) * (1.0 / np.sqrt(H)) / s[:, None]
    up_stack = np.random.standard_normal((E, H, F)) * (1.0 / np.sqrt(H)) / s[:, None] * t
    down_stack = np.random.standard_normal((E, F, H)) * (1.5 / np.sqrt(F)) / t[:, None]
    gate_words, gate_scales = pack_weight(gate_stack.reshape(-1, F), "e4m3")
    up_words, up_scales = pack_weight(up_stack.reshape(-1, F), "e4m3")
    down_words, down_scales = pack_weight(down_stack.reshape(-1, H), "e4m3")
    return {"hidden_states": hidden_states,
            "gate_w_words": gate_words, "gate_w_scales": gate_scales,
            "up_w_words": up_words, "up_w_scales": up_scales,
            "down_w_words": down_words, "down_w_scales": down_scales}


def reference(hidden_states, gate_w_words, gate_w_scales, up_w_words, up_w_scales, down_w_words, down_w_scales):
    x = f64(hidden_states).reshape(E, -1, H)
    xq = mxq(x, 2, "e4m3")
    gate = xq @ unpack_weight(gate_w_words, gate_w_scales, "e4m3").reshape(E, H, F)
    up = xq @ unpack_weight(up_w_words, up_w_scales, "e4m3").reshape(E, H, F)
    h = up * silu(gate)
    out = mxq(h, 2, "e4m3") @ unpack_weight(down_w_words, down_w_scales, "e4m3").reshape(E, F, H)
    return out.reshape(-1, H)

@@ -1,0 +1,184 @@
+from contextlib import ExitStack
+
+import concourse.mybir as mybir
+from concourse.masks import make_identity
+
+F32 = mybir.dt.float32
+BF16 = mybir.dt.bfloat16
+I32 = mybir.dt.int32
+U32 = mybir.dt.uint32
+U8 = mybir.dt.uint8
+FP8X4 = mybir.dt.float8_e4m3fn_x4
+
+P = 128
+PACK = 4
+K_PASS = P * PACK
+EXPERTS = 2
+WIDTH = 2048
+GROUPS = WIDTH // K_PASS
+BANK = 512
+BANKS = WIDTH // BANK
+QUADRANT = 32
+LIVE_ROWS = PACK * GROUPS
+
+FLOPS = 2 * EXPERTS * P * 3 * WIDTH * WIDTH
+
+
+def load_scale_planes(nc, pool, scales, expert, name):
+    planes = pool.tile([P, WIDTH], U8, name=name, align_bytes=64)
+    nc.vector.memset(planes[:].bitcast(I32), 0)
+    groups = slice(GROUPS * expert, GROUPS * (expert + 1))
+    for quadrant in range(P // QUADRANT):
+        first = QUADRANT * quadrant
+        nc.sync.dma_start(
+            out=planes[first : first + LIVE_ROWS, :].bitcast(I32),
+            in_=scales[groups, PACK * quadrant : PACK * (quadrant + 1), :].bitcast(I32),
+        )
+    return planes
+
+
+def load_words(nc, pool, words, group, pieces):
+    chunk = pool.tile([P, WIDTH], U32, tag="words", align_bytes=64)
+    source = words[group].rearrange("p n t -> p (n t)").bitcast(I32)
+    width = WIDTH // pieces
+    for piece in range(pieces):
+        cols = slice(piece * width, (piece + 1) * width)
+        nc.sync.dma_start(out=chunk[:, cols].bitcast(I32), in_=source[:, cols])
+    return chunk
+
+
+def quantise_tokens(nc, pool, psum, identity, tokens):
+    pairs = tokens[:].bitcast(F32)
+    grouped = pool.tile([P, GROUPS, P, PACK], BF16, align_bytes=64)
+    codes = pool.tile([P, GROUPS * P], U32, align_bytes=64)
+    scales = pool.tile([P, GROUPS * P], U8, align_bytes=64)
+    per_bank = BANK // (2 * P)
+    for first in range(0, GROUPS, per_bank):
+        turned = psum.tile([P, per_bank, 2, P], F32, tag="bank")
+        for i in range(per_bank):
+            start = (first + i) * (K_PASS // 2)
+            for u in range(2):
+                nc.tensor.transpose(
+                    turned[:, i, u, :], pairs[:, start + u : start + K_PASS // 2 : 2], identity[:]
+                )
+        nc.vector.tensor_copy(
+            out=grouped[:, first : first + per_bank, :, :].bitcast(F32),
+            in_=turned[:].rearrange("p g u r -> p g r u"),
+        )
+        cols = slice(first * P, (first + per_bank) * P)
+        nc.vector.quantize_mx(
+            out=codes[:, cols].bitcast(FP8X4),
+            scales=scales[:, cols],
+            in_=grouped[:, first : first + per_bank, :, :].rearrange("p g r t -> p (g r t)"),
+        )
+    return codes, scales
+
+
+def multiply_group(nc, banks, tokens_q, chunk, planes, group):
+    codes, scales = tokens_q
+    stationary = slice(group * P, (group + 1) * P)
+    for j in range(BANKS):
+        cols = slice(j * BANK, (j + 1) * BANK)
+        nc.tensor.matmul_mx(
+            out=banks[j][:],
+            lhsT=codes[:, stationary].bitcast(FP8X4),
+            lhsT_scale=scales[:, stationary],
+            rhs=chunk[:, cols].bitcast(FP8X4),
+            rhs_scale=planes[PACK * group : P, cols],
+            start=(group == 0),
+            stop=(group == GROUPS - 1),
+        )
+
+
+def tile_llama4textexperts_w_e_kernel(
+    tc,
+    hidden_states,
+    gate_w_words,
+    gate_w_scales,
+    up_w_words,
+    up_w_scales,
+    down_w_words,
+    down_w_scales,
+    out,
+):
+    nc = tc.nc
+    with ExitStack() as ctx:
+        const = ctx.enter_context(tc.tile_pool(name="const", bufs=1))
+        weights = ctx.enter_context(tc.tile_pool(name="weights", bufs=3 * GROUPS))
+        acts = ctx.enter_context(tc.tile_pool(name="acts", bufs=2))
+        work = ctx.enter_context(tc.tile_pool(name="work", bufs=BANKS))
+        psum = ctx.enter_context(tc.psum_pool(name="psum", bufs=8))
+
+        def product_banks(name):
+            return [
+                psum.tile([P, BANK], F32, tag="bank", name="%s%d" % (name, j)) for j in range(BANKS)
+            ]
+
+        def load_first_layer(expert):
+            return [
+                (
+                    load_words(nc, weights, gate_w_words, GROUPS * expert + g, 1),
+                    load_words(nc, weights, up_w_words, GROUPS * expert + g, 1),
+                )
+                for g in range(GROUPS)
+            ]
+
+        def load_second_layer(expert):
+            return [
+                load_words(nc, weights, down_w_words, GROUPS * expert + g, BANKS if g == GROUPS - 1 else 1)
+                for g in range(GROUPS)
+            ]
+
+        identity = const.tile([P, P], F32)
+        make_identity(nc, identity[:])
+
+        x = []
+        for expert in range(EXPERTS):
+            x_tile = acts.tile([P, WIDTH], BF16, tag="tokens")
+            nc.sync.dma_start(out=x_tile[:], in_=hidden_states[expert * P : (expert + 1) * P, :])
+            x.append(x_tile)
+        gate_planes, up_planes, down_planes = [], [], []
+        for expert in range(EXPERTS):
+            gate_planes.append(load_scale_planes(nc, const, gate_w_scales, expert, "gate_planes%d" % expert))
+            up_planes.append(load_scale_planes(nc, const, up_w_scales, expert, "up_planes%d" % expert))
+            down_planes.append(load_scale_planes(nc, const, down_w_scales, expert, "down_planes%d" % expert))
+        first_layer = load_first_layer(0)
+        second_layer = load_second_layer(0)
+
+        x_q = [quantise_tokens(nc, acts, psum, identity, x[expert]) for expert in range(EXPERTS)]
+
+        for expert in range(EXPERTS):
+            following = expert + 1
+
+            gate = product_banks("gate")
+            up = product_banks("up")
+            for g in range(GROUPS):
+                gate_chunk, up_chunk = first_layer[g]
+                multiply_group(nc, gate, x_q[expert], gate_chunk, gate_planes[expert], g)
+                multiply_group(nc, up, x_q[expert], up_chunk, up_planes[expert], g)
+            if following < EXPERTS:
+                first_layer = load_first_layer(following)
+
+            h = acts.tile([P, WIDTH], BF16, tag="tokens")
+            for j in range(BANKS):
+                silu = work.tile([P, BANK], F32)
+                nc.scalar.activation(out=silu[:], in_=gate[j][:], func=mybir.ActivationFunctionType.Silu)
+                nc.vector.tensor_tensor(
+                    out=h[:, j * BANK : (j + 1) * BANK], in0=up[j][:], in1=silu[:], op=mybir.AluOpType.mult
+                )
+            h_q = quantise_tokens(nc, acts, psum, identity, h)
+
+            product = product_banks("product")
+            for g in range(GROUPS):
+                multiply_group(nc, product, h_q, second_layer[g], down_planes[expert], g)
+            if following < EXPERTS:
+                second_layer = load_second_layer(following)
+
+            result = acts.tile([P, WIDTH], F32)
+            for j in range(BANKS):
+                cols = slice(j * BANK, (j + 1) * BANK)
+                if j % 2 == 0:
+                    nc.scalar.copy(out=result[:, cols], in_=product[j][:])
+                else:
+                    nc.vector.tensor_copy(out=result[:, cols], in_=product[j][:])
+                nc.sync.dma_start(out=out[expert * P : (expert + 1) * P, cols], in_=result[:, cols])

@@ -30,9 +30,9 @@ def load_scale_planes(nc, pool, scales, expert, name):
     groups = slice(GROUPS * expert, GROUPS * (expert + 1))
     for quadrant in range(P // QUADRANT):
         first = QUADRANT * quadrant
-        nc.sync.dma_start(
-            out=planes[first : first + LIVE_ROWS, :].bitcast(I32),
-            in_=scales[groups, PACK * quadrant : PACK * (quadrant + 1), :].bitcast(I32),
+        nc.gpsimd.dma_start(
+            out=planes[first : first + LIVE_ROWS, :].bitcast(F32),
+            in_=scales[groups, PACK * quadrant : PACK * (quadrant + 1), :].bitcast(F32),
         )
     return planes
 

@@ -20,6 +20,7 @@ BANK = 512
 BANKS = WIDTH // BANK
 QUADRANT = 32
 LIVE_ROWS = PACK * GROUPS
+PIECES = 2
 
 FLOPS = 2 * EXPERTS * P * 3 * WIDTH * WIDTH
 
@@ -108,6 +109,7 @@ def tile_llama4textexperts_w_e_kernel(
         acts = ctx.enter_context(tc.tile_pool(name="acts", bufs=2))
         work = ctx.enter_context(tc.tile_pool(name="work", bufs=BANKS))
         psum = ctx.enter_context(tc.psum_pool(name="psum", bufs=8))
+        ctx.enter_context(tc.manual_schedule())
 
         def product_banks(name):
             return [
@@ -125,7 +127,7 @@ def tile_llama4textexperts_w_e_kernel(
 
         def load_second_layer(expert):
             return [
-                load_words(nc, weights, down_w_words, GROUPS * expert + g, BANKS if g == GROUPS - 1 else 1)
+                load_words(nc, weights, down_w_words, GROUPS * expert + g, PIECES if g == GROUPS - 1 else 1)
                 for g in range(GROUPS)
             ]
 
@@ -181,4 +183,6 @@ def tile_llama4textexperts_w_e_kernel(
                     nc.scalar.copy(out=result[:, cols], in_=product[j][:])
                 else:
                     nc.vector.tensor_copy(out=result[:, cols], in_=product[j][:])
+            for piece in range(PIECES):
+                cols = slice(piece * (WIDTH // PIECES), (piece + 1) * (WIDTH // PIECES))
                 nc.sync.dma_start(out=out[expert * P : (expert + 1) * P, cols], in_=result[:, cols])

@@ -105,7 +105,7 @@ def tile_llama4textexperts_w_e_kernel(
     nc = tc.nc
     with ExitStack() as ctx:
         const = ctx.enter_context(tc.tile_pool(name="const", bufs=1))
-        weights = ctx.enter_context(tc.tile_pool(name="weights", bufs=3 * GROUPS))
+        weights = ctx.enter_context(tc.tile_pool(name="weights", bufs=2 * GROUPS * EXPERTS))
         acts = ctx.enter_context(tc.tile_pool(name="acts", bufs=2))
         work = ctx.enter_context(tc.tile_pool(name="work", bufs=BANKS))
         psum = ctx.enter_context(tc.psum_pool(name="psum", bufs=8))
@@ -143,23 +143,21 @@ def tile_llama4textexperts_w_e_kernel(
         for expert in range(EXPERTS):
             gate_planes.append(load_scale_planes(nc, const, gate_w_scales, expert, "gate_planes%d" % expert))
             up_planes.append(load_scale_planes(nc, const, up_w_scales, expert, "up_planes%d" % expert))
+        for expert in range(EXPERTS):
             down_planes.append(load_scale_planes(nc, const, down_w_scales, expert, "down_planes%d" % expert))
-        first_layer = load_first_layer(0)
-        second_layer = load_second_layer(0)
+        first_layer = [load_first_layer(expert) for expert in range(EXPERTS)]
 
         x_q = [quantise_tokens(nc, acts, psum, identity, x[expert]) for expert in range(EXPERTS)]
 
+        second_layer, h_q = [], []
         for expert in range(EXPERTS):
-            following = expert + 1
-
             gate = product_banks("gate")
             up = product_banks("up")
             for g in range(GROUPS):
-                gate_chunk, up_chunk = first_layer[g]
+                gate_chunk, up_chunk = first_layer[expert][g]
                 multiply_group(nc, gate, x_q[expert], gate_chunk, gate_planes[expert], g)
                 multiply_group(nc, up, x_q[expert], up_chunk, up_planes[expert], g)
-            if following < EXPERTS:
-                first_layer = load_first_layer(following)
+            second_layer.append(load_second_layer(expert))
 
             h = acts.tile([P, WIDTH], BF16, tag="tokens")
             for j in range(BANKS):
@@ -168,13 +166,12 @@ def tile_llama4textexperts_w_e_kernel(
                 nc.vector.tensor_tensor(
                     out=h[:, j * BANK : (j + 1) * BANK], in0=up[j][:], in1=silu[:], op=mybir.AluOpType.mult
                 )
-            h_q = quantise_tokens(nc, acts, psum, identity, h)
+            h_q.append(quantise_tokens(nc, acts, psum, identity, h))
 
+        for expert in range(EXPERTS):
             product = product_banks("product")
             for g in range(GROUPS):
-                multiply_group(nc, product, h_q, second_layer[g], down_planes[expert], g)
-            if following < EXPERTS:
-                second_layer = load_second_layer(following)
+                multiply_group(nc, product, h_q[expert], second_layer[expert][g], down_planes[expert], g)
 
             result = acts.tile([P, WIDTH], F32)
             for j in range(BANKS):

@@ -21,6 +21,7 @@ BANKS = WIDTH // BANK
 QUADRANT = 32
 LIVE_ROWS = PACK * GROUPS
 PIECES = 2
+SPAN = 2
 
 FLOPS = 2 * EXPERTS * P * 3 * WIDTH * WIDTH
 
@@ -38,13 +39,19 @@ def load_scale_planes(nc, pool, scales, expert, name):
     return planes
 
 
-def load_words(nc, pool, words, group, pieces):
-    chunk = pool.tile([P, WIDTH], U32, tag="words", align_bytes=64)
-    source = words[group].rearrange("p n t -> p (n t)").bitcast(I32)
-    width = WIDTH // pieces
-    for piece in range(pieces):
+def load_words(nc, pool, words, first, fine_end=False):
+    chunk = pool.tile([P, SPAN, WIDTH], U32, tag="words", align_bytes=64)
+    source = words[first : first + SPAN].rearrange("g p n t -> p g (n t)").bitcast(I32)
+    target = chunk[:].bitcast(I32)
+    if not fine_end:
+        nc.sync.dma_start(out=target, in_=source)
+        return chunk
+    last = SPAN - 1
+    nc.sync.dma_start(out=target[:, :last, :], in_=source[:, :last, :])
+    width = WIDTH // PIECES
+    for piece in range(PIECES):
         cols = slice(piece * width, (piece + 1) * width)
-        nc.sync.dma_start(out=chunk[:, cols].bitcast(I32), in_=source[:, cols])
+        nc.sync.dma_start(out=target[:, last, cols], in_=source[:, last, cols])
     return chunk
 
 
@@ -84,7 +91,7 @@ def multiply_group(nc, banks, tokens_q, chunk, planes, group):
             out=banks[j][:],
             lhsT=codes[:, stationary].bitcast(FP8X4),
             lhsT_scale=scales[:, stationary],
-            rhs=chunk[:, cols].bitcast(FP8X4),
+            rhs=chunk[:, group % SPAN, cols].bitcast(FP8X4),
             rhs_scale=planes[PACK * group : P, cols],
             start=(group == 0),
             stop=(group == GROUPS - 1),
@@ -105,7 +112,7 @@ def tile_llama4textexperts_w_e_kernel(
     nc = tc.nc
     with ExitStack() as ctx:
         const = ctx.enter_context(tc.tile_pool(name="const", bufs=1))
-        weights = ctx.enter_context(tc.tile_pool(name="weights", bufs=2 * GROUPS * EXPERTS))
+        weights = ctx.enter_context(tc.tile_pool(name="weights", bufs=2 * GROUPS * EXPERTS // SPAN))
         acts = ctx.enter_context(tc.tile_pool(name="acts", bufs=2))
         work = ctx.enter_context(tc.tile_pool(name="work", bufs=BANKS))
         psum = ctx.enter_context(tc.psum_pool(name="psum", bufs=8))
@@ -119,16 +126,22 @@ def tile_llama4textexperts_w_e_kernel(
         def load_first_layer(expert):
             return [
                 (
-                    load_words(nc, weights, gate_w_words, GROUPS * expert + g, 1),
-                    load_words(nc, weights, up_w_words, GROUPS * expert + g, 1),
+                    load_words(nc, weights, gate_w_words, GROUPS * expert + g),
+                    load_words(nc, weights, up_w_words, GROUPS * expert + g),
                 )
-                for g in range(GROUPS)
+                for g in range(0, GROUPS, SPAN)
             ]
 
         def load_second_layer(expert):
             return [
-                load_words(nc, weights, down_w_words, GROUPS * expert + g, PIECES if g == GROUPS - 1 else 1)
-                for g in range(GROUPS)
+                load_words(
+                    nc,
+                    weights,
+                    down_w_words,
+                    GROUPS * expert + g,
+                    fine_end=(expert == EXPERTS - 1 and g == GROUPS - SPAN),
+                )
+                for g in range(0, GROUPS, SPAN)
             ]
 
         identity = const.tile([P, P], F32)
@@ -154,7 +167,7 @@ def tile_llama4textexperts_w_e_kernel(
             gate = product_banks("gate")
             up = product_banks("up")
             for g in range(GROUPS):
-                gate_chunk, up_chunk = first_layer[expert][g]
+                gate_chunk, up_chunk = first_layer[expert][g // SPAN]
                 multiply_group(nc, gate, x_q[expert], gate_chunk, gate_planes[expert], g)
                 multiply_group(nc, up, x_q[expert], up_chunk, up_planes[expert], g)
             second_layer.append(load_second_layer(expert))
@@ -171,7 +184,7 @@ def tile_llama4textexperts_w_e_kernel(
         for expert in range(EXPERTS):
             product = product_banks("product")
             for g in range(GROUPS):
-                multiply_group(nc, product, h_q[expert], second_layer[expert][g], down_planes[expert], g)
+                multiply_group(nc, product, h_q[expert], second_layer[expert][g // SPAN], down_planes[expert], g)
 
             result = acts.tile([P, WIDTH], F32)
             for j in range(BANKS):

@@ -20,7 +20,7 @@ BANK = 512
 BANKS = WIDTH // BANK
 QUADRANT = 32
 LIVE_ROWS = PACK * GROUPS
-PIECES = 2
+PIECES = 4
 SPAN = 2
 
 FLOPS = 2 * EXPERTS * P * 3 * WIDTH * WIDTH
@@ -193,6 +193,8 @@ def tile_llama4textexperts_w_e_kernel(
                     nc.scalar.copy(out=result[:, cols], in_=product[j][:])
                 else:
                     nc.vector.tensor_copy(out=result[:, cols], in_=product[j][:])
-            for piece in range(PIECES):
-                cols = slice(piece * (WIDTH // PIECES), (piece + 1) * (WIDTH // PIECES))
+            pieces = PIECES if expert == EXPERTS - 1 else 1
+            width = WIDTH // pieces
+            for piece in range(pieces):
+                cols = slice(piece * width, (piece + 1) * width)
                 nc.sync.dma_start(out=out[expert * P : (expert + 1) * P, cols], in_=result[:, cols])

@@ -20,6 +20,7 @@ BANK = 512
 BANKS = WIDTH // BANK
 QUADRANT = 32
 LIVE_ROWS = PACK * GROUPS
+BURST = 256
 PIECES = 4
 SPAN = 2
 
@@ -27,7 +28,7 @@ FLOPS = 2 * EXPERTS * P * 3 * WIDTH * WIDTH
 
 
 def load_scale_planes(nc, pool, scales, expert, name):
-    planes = pool.tile([P, WIDTH], U8, name=name, align_bytes=64)
+    planes = pool.tile([P, WIDTH], U8, name=name, align_bytes=BURST)
     nc.vector.memset(planes[:].bitcast(I32), 0)
     groups = slice(GROUPS * expert, GROUPS * (expert + 1))
     for quadrant in range(P // QUADRANT):
@@ -40,7 +41,7 @@ def load_scale_planes(nc, pool, scales, expert, name):
 
 
 def load_words(nc, pool, words, first, fine_end=False):
-    chunk = pool.tile([P, SPAN, WIDTH], U32, tag="words", align_bytes=64)
+    chunk = pool.tile([P, SPAN, WIDTH], U32, tag="words", align_bytes=BURST)
     source = words[first : first + SPAN].rearrange("g p n t -> p g (n t)").bitcast(I32)
     target = chunk[:].bitcast(I32)
     if not fine_end:
@@ -149,7 +150,7 @@ def tile_llama4textexperts_w_e_kernel(
 
         x = []
         for expert in range(EXPERTS):
-            x_tile = acts.tile([P, WIDTH], BF16, tag="tokens")
+            x_tile = acts.tile([P, WIDTH], BF16, tag="tokens", align_bytes=BURST)
             nc.sync.dma_start(out=x_tile[:], in_=hidden_states[expert * P : (expert + 1) * P, :])
             x.append(x_tile)
         gate_planes, up_planes, down_planes = [], [], []
@@ -172,7 +173,7 @@ def tile_llama4textexperts_w_e_kernel(
                 multiply_group(nc, up, x_q[expert], up_chunk, up_planes[expert], g)
             second_layer.append(load_second_layer(expert))
 
-            h = acts.tile([P, WIDTH], BF16, tag="tokens")
+            h = acts.tile([P, WIDTH], BF16, tag="tokens", align_bytes=BURST)
             for j in range(BANKS):
                 silu = work.tile([P, BANK], F32)
                 nc.scalar.activation(out=silu[:], in_=gate[j][:], func=mybir.ActivationFunctionType.Silu)
@@ -186,7 +187,7 @@ def tile_llama4textexperts_w_e_kernel(
             for g in range(GROUPS):
                 multiply_group(nc, product, h_q[expert], second_layer[expert][g // SPAN], down_planes[expert], g)
 
-            result = acts.tile([P, WIDTH], F32)
+            result = acts.tile([P, WIDTH], F32, align_bytes=BURST)
             for j in range(BANKS):
                 cols = slice(j * BANK, (j + 1) * BANK)
                 if j % 2 == 0:

from contextlib import ExitStack

import concourse.mybir as mybir
from concourse.masks import make_identity

F32 = mybir.dt.float32
BF16 = mybir.dt.bfloat16
I32 = mybir.dt.int32
U32 = mybir.dt.uint32
U8 = mybir.dt.uint8
FP8X4 = mybir.dt.float8_e4m3fn_x4

P = 128
PACK = 4
K_PASS = P * PACK
EXPERTS = 2
WIDTH = 2048
GROUPS = WIDTH // K_PASS
BANK = 512
BANKS = WIDTH // BANK
QUADRANT = 32
LIVE_ROWS = PACK * GROUPS
BURST = 256
PIECES = 4
SPAN = 2

FLOPS = 2 * EXPERTS * P * 3 * WIDTH * WIDTH


def load_scale_planes(nc, pool, scales, expert, name):
    planes = pool.tile([P, WIDTH], U8, name=name, align_bytes=BURST)
    nc.vector.memset(planes[:].bitcast(I32), 0)
    groups = slice(GROUPS * expert, GROUPS * (expert + 1))
    for quadrant in range(P // QUADRANT):
        first = QUADRANT * quadrant
        nc.gpsimd.dma_start(
            out=planes[first : first + LIVE_ROWS, :].bitcast(F32),
            in_=scales[groups, PACK * quadrant : PACK * (quadrant + 1), :].bitcast(F32),
        )
    return planes


def load_words(nc, pool, words, first, fine_end=False):
    chunk = pool.tile([P, SPAN, WIDTH], U32, tag="words", align_bytes=BURST)
    source = words[first : first + SPAN].rearrange("g p n t -> p g (n t)").bitcast(I32)
    target = chunk[:].bitcast(I32)
    if not fine_end:
        nc.sync.dma_start(out=target, in_=source)
        return chunk
    last = SPAN - 1
    nc.sync.dma_start(out=target[:, :last, :], in_=source[:, :last, :])
    width = WIDTH // PIECES
    for piece in range(PIECES):
        cols = slice(piece * width, (piece + 1) * width)
        nc.sync.dma_start(out=target[:, last, cols], in_=source[:, last, cols])
    return chunk


def quantise_tokens(nc, pool, psum, identity, tokens):
    pairs = tokens[:].bitcast(F32)
    grouped = pool.tile([P, GROUPS, P, PACK], BF16, align_bytes=64)
    codes = pool.tile([P, GROUPS * P], U32, align_bytes=64)
    scales = pool.tile([P, GROUPS * P], U8, align_bytes=64)
    per_bank = BANK // (2 * P)
    for first in range(0, GROUPS, per_bank):
        turned = psum.tile([P, per_bank, 2, P], F32, tag="bank")
        for i in range(per_bank):
            start = (first + i) * (K_PASS // 2)
            for u in range(2):
                nc.tensor.transpose(
                    turned[:, i, u, :], pairs[:, start + u : start + K_PASS // 2 : 2], identity[:]
                )
        nc.vector.tensor_copy(
            out=grouped[:, first : first + per_bank, :, :].bitcast(F32),
            in_=turned[:].rearrange("p g u r -> p g r u"),
        )
        cols = slice(first * P, (first + per_bank) * P)
        nc.vector.quantize_mx(
            out=codes[:, cols].bitcast(FP8X4),
            scales=scales[:, cols],
            in_=grouped[:, first : first + per_bank, :, :].rearrange("p g r t -> p (g r t)"),
        )
    return codes, scales


def multiply_group(nc, banks, tokens_q, chunk, planes, group):
    codes, scales = tokens_q
    stationary = slice(group * P, (group + 1) * P)
    for j in range(BANKS):
        cols = slice(j * BANK, (j + 1) * BANK)
        nc.tensor.matmul_mx(
            out=banks[j][:],
            lhsT=codes[:, stationary].bitcast(FP8X4),
            lhsT_scale=scales[:, stationary],
            rhs=chunk[:, group % SPAN, cols].bitcast(FP8X4),
            rhs_scale=planes[PACK * group : P, cols],
            start=(group == 0),
            stop=(group == GROUPS - 1),
        )


def tile_llama4textexperts_w_e_kernel(
    tc,
    hidden_states,
    gate_w_words,
    gate_w_scales,
    up_w_words,
    up_w_scales,
    down_w_words,
    down_w_scales,
    out,
):
    nc = tc.nc
    with ExitStack() as ctx:
        const = ctx.enter_context(tc.tile_pool(name="const", bufs=1))
        weights = ctx.enter_context(tc.tile_pool(name="weights", bufs=2 * GROUPS * EXPERTS // SPAN))
        acts = ctx.enter_context(tc.tile_pool(name="acts", bufs=2))
        work = ctx.enter_context(tc.tile_pool(name="work", bufs=BANKS))
        psum = ctx.enter_context(tc.psum_pool(name="psum", bufs=8))
        ctx.enter_context(tc.manual_schedule())

        def product_banks(name):
            return [
                psum.tile([P, BANK], F32, tag="bank", name="%s%d" % (name, j)) for j in range(BANKS)
            ]

        def load_first_layer(expert):
            return [
                (
                    load_words(nc, weights, gate_w_words, GROUPS * expert + g),
                    load_words(nc, weights, up_w_words, GROUPS * expert + g),
                )
                for g in range(0, GROUPS, SPAN)
            ]

        def load_second_layer(expert):
            return [
                load_words(
                    nc,
                    weights,
                    down_w_words,
                    GROUPS * expert + g,
                    fine_end=(expert == EXPERTS - 1 and g == GROUPS - SPAN),
                )
                for g in range(0, GROUPS, SPAN)
            ]

        identity = const.tile([P, P], F32)
        make_identity(nc, identity[:])

        x = []
        for expert in range(EXPERTS):
            x_tile = acts.tile([P, WIDTH], BF16, tag="tokens", align_bytes=BURST)
            nc.sync.dma_start(out=x_tile[:], in_=hidden_states[expert * P : (expert + 1) * P, :])
            x.append(x_tile)
        gate_planes, up_planes, down_planes = [], [], []
        for expert in range(EXPERTS):
            gate_planes.append(load_scale_planes(nc, const, gate_w_scales, expert, "gate_planes%d" % expert))
            up_planes.append(load_scale_planes(nc, const, up_w_scales, expert, "up_planes%d" % expert))
        for expert in range(EXPERTS):
            down_planes.append(load_scale_planes(nc, const, down_w_scales, expert, "down_planes%d" % expert))
        first_layer = [load_first_layer(expert) for expert in range(EXPERTS)]

        x_q = [quantise_tokens(nc, acts, psum, identity, x[expert]) for expert in range(EXPERTS)]

        second_layer, h_q = [], []
        for expert in range(EXPERTS):
            gate = product_banks("gate")
            up = product_banks("up")
            for g in range(GROUPS):
                gate_chunk, up_chunk = first_layer[expert][g // SPAN]
                multiply_group(nc, gate, x_q[expert], gate_chunk, gate_planes[expert], g)
                multiply_group(nc, up, x_q[expert], up_chunk, up_planes[expert], g)
            second_layer.append(load_second_layer(expert))

            h = acts.tile([P, WIDTH], BF16, tag="tokens", align_bytes=BURST)
            for j in range(BANKS):
                silu = work.tile([P, BANK], F32)
                nc.scalar.activation(out=silu[:], in_=gate[j][:], func=mybir.ActivationFunctionType.Silu)
                nc.vector.tensor_tensor(
                    out=h[:, j * BANK : (j + 1) * BANK], in0=up[j][:], in1=silu[:], op=mybir.AluOpType.mult
                )
            h_q.append(quantise_tokens(nc, acts, psum, identity, h))

        for expert in range(EXPERTS):
            product = product_banks("product")
            for g in range(GROUPS):
                multiply_group(nc, product, h_q[expert], second_layer[expert][g // SPAN], down_planes[expert], g)

            result = acts.tile([P, WIDTH], F32, align_bytes=BURST)
            for j in range(BANKS):
                cols = slice(j * BANK, (j + 1) * BANK)
                if j % 2 == 0:
                    nc.scalar.copy(out=result[:, cols], in_=product[j][:])
                else:
                    nc.vector.tensor_copy(out=result[:, cols], in_=product[j][:])
            pieces = PIECES if expert == EXPERTS - 1 else 1
            width = WIDTH // pieces
            for piece in range(pieces):
                cols = slice(piece * width, (piece + 1) * width)
                nc.sync.dma_start(out=out[expert * P : (expert + 1) * P, cols], in_=result[:, cols])
